import numpy as np
import ml_dtypes


def mxq(x, axis, fmt="e4m3"):
    dtype, down = {"e4m3": (ml_dtypes.float8_e4m3fn, 7), "e5m2": (ml_dtypes.float8_e5m2, 14)}[fmt]
    v = np.moveaxis(np.asarray(x, np.float32).astype(ml_dtypes.bfloat16).astype(np.float64), axis, -1)
    blocks = v.reshape(v.shape[:-1] + (-1, 32))
    amax = np.abs(blocks).max(-1, keepdims=True)
    byte = np.maximum(np.where(amax > 0, np.frexp(amax)[1] - 1 + 127, 0) - down, 1)
    scale = np.exp2(byte - 127.0)
    codes = (blocks / scale).astype(np.float32).astype(dtype).astype(np.float64)
    return np.moveaxis((codes * scale).reshape(v.shape), -1, axis)


WIDE = False


def mx_kscale(k):
    if not WIDE:
        return np.ones(k)
    levels = np.array([10, -10, 5, -5, 0])
    if k % 512:
        return np.exp2(np.random.permutation(np.resize(levels, k // 32))).repeat(32)
    a = np.empty((k // 512, 16))
    for p in range(k // 512):
        a[p, :8] = np.random.permutation(np.resize(levels, 8))
        for g in range(8):
            far = levels[np.abs(levels - a[p, g]) >= 10]
            a[p, g + 8] = far[np.random.randint(len(far))]
    return np.exp2(a.ravel()).repeat(32)


BF16 = ml_dtypes.bfloat16


def bf(x):
    return np.asarray(x, np.float32).astype(BF16)


def f64(x):
    return np.asarray(x).astype(np.float64)


B, S, H, NH, HS, ROT = 4, 64, 2560, 32, 80, 32
T = B * S
E = NH * HS
R2 = ROT // 2
ROPE_BASE = 10000.0


def rope_partial(x, cos, sin):
    xr, xp = x[..., :ROT], x[..., ROT:]
    x1, x2 = xr[..., :R2], xr[..., R2:]
    c, s = cos[:, None, :], sin[:, None, :]
    rot = np.concatenate([x1 * c - x2 * s, x2 * c + x1 * s], axis=-1)
    return np.concatenate([rot, xp], axis=-1)


def draw0():
    s = mx_kscale(H)
    inv_freq = 1.0 / ROPE_BASE ** (np.arange(0, ROT, 2) / ROT)
    pos = np.tile(np.arange(S), B)
    freqs = pos[:, None] * inv_freq[None, :]
    return {"hidden_states": bf(np.random.standard_normal((T, H)) * s),
            "cos": bf(np.cos(freqs)),
            "sin": bf(np.sin(freqs)),
            "w_qk": bf(np.random.standard_normal((2 * E, H)) / np.sqrt(H) / s[None, :]),
            "b_qk": bf(np.random.standard_normal(2 * E) * 0.3)}


def core(hidden_states, cos, sin, w_qk, b_qk):
    qk = (mxq(f64(hidden_states), 1, "e4m3") @ mxq(f64(w_qk), 1, "e4m3").T) + f64(b_qk)
    q = qk[:, :E].reshape(T, NH, HS)
    k = qk[:, E:].reshape(T, NH, HS)
    c, s = f64(cos), f64(sin)
    return rope_partial(q, c, s), rope_partial(k, c, s)


def e4m3fn_bytes(y):
    return np.clip(np.asarray(y, np.float64), -448.0, 448.0).astype(np.float32).astype(ml_dtypes.float8_e4m3fn).view(np.uint8)


def e4m3fn_values(b):
    return np.asarray(b, np.uint8).view(ml_dtypes.float8_e4m3fn).astype(np.float64)


def setup_inputs():
    d = draw0()
    x0 = np.asarray(d['w_qk']).astype(np.float64)
    s = (np.max(np.abs(x0), axis=(0,), keepdims=True) / 448.0).astype(np.float32)
    out = {}
    for k, v in d.items():
        if k == 'w_qk':
            out['w_qk_bytes'] = e4m3fn_bytes(x0 / s.astype(np.float64))
            out['w_qk_scale'] = s
        else:
            out[k] = v
    return out


def reference(hidden_states, cos, sin, w_qk_bytes, w_qk_scale, b_qk):
    return core(hidden_states, cos, sin, e4m3fn_values(w_qk_bytes) * w_qk_scale.astype(np.float64), b_qk)

@@ -1,0 +1,312 @@
+from contextlib import ExitStack
+
+import concourse.mybir as mybir
+from concourse.masks import make_identity
+
+F32 = mybir.dt.float32
+BF16 = mybir.dt.bfloat16
+U32 = mybir.dt.uint32
+U8 = mybir.dt.uint8
+FP8 = mybir.dt.float8_e4m3fn
+FP8X4 = mybir.dt.float8_e4m3fn_x4
+ALU = mybir.AluOpType
+ACT = mybir.ActivationFunctionType
+
+P = 128
+TOKENS = 256
+K = 2560
+CHANNELS = 5120
+HALF = 2560
+HEAD = 80
+ROT = 32
+PASSES = 5
+N_TILE = 512
+TILES = 10
+FLOPS = 2 * TOKENS * K * CHANNELS
+
+NVB = [(4, 4), (4, 3)] * 5
+ROPE_AFTER = [1, 3, 4]
+
+
+def head_end(i):
+    return (N_TILE * (i + 1) - ROT) // HEAD + 1
+
+
+def tile_flashphiattention_pa_kernel(
+    tc, hidden_states, cos, sin, w_qk_bytes, w_qk_scale, b_qk, out_0, out_1
+):
+    nc = tc.nc
+    with ExitStack() as ctx:
+        const = ctx.enter_context(tc.tile_pool(name="const", bufs=1))
+        bytes_pool = ctx.enter_context(tc.tile_pool(name="bytes", bufs=3))
+        wide_pool = ctx.enter_context(tc.tile_pool(name="wide", bufs=8))
+        grouped_pool = ctx.enter_context(tc.tile_pool(name="grouped", bufs=4))
+        code_pool = ctx.enter_context(tc.tile_pool(name="codes", bufs=3))
+        tmp_pool = ctx.enter_context(tc.tile_pool(name="tmp", bufs=2))
+        psum_t = ctx.enter_context(tc.psum_pool(name="psum_t", bufs=4))
+        psum_a = ctx.enter_context(tc.psum_pool(name="psum_a", bufs=2))
+        ctx.enter_context(tc.manual_schedule(engines={mybir.EngineType.SP}))
+
+        scale_b = const.tile([P, K], F32, name="scale_b")
+        sc4 = const.tile([P, PASSES, 4], F32, name="sc4")
+        bias_b = const.tile([P, CHANNELS], BF16, name="bias_b")
+        cs_raw = const.tile([P, 2, 2, 16], BF16, name="cs_raw")
+        cc = const.tile([P, 2, ROT], F32, name="cc")
+        ss = const.tile([P, 2, ROT], F32, name="ss")
+        ident = const.tile([P, P], F32, name="ident")
+        junk = const.tile([P, 2], F32, name="junk")
+        h_sb = const.tile([P, 2, K], BF16, name="h_sb")
+        h_codes = const.tile([P, PASSES, TOKENS], U32, name="h_codes", align_bytes=64)
+        h_scales = const.tile([P, PASSES, TOKENS], U8, name="h_scales", align_bytes=64)
+        x_out = const.tile([P, 2, CHANNELS], F32, name="x_out")
+
+        w_bytes = {}
+        w_wide = {}
+        grouped = {}
+        codes = {}
+        acc = {}
+
+        def load(j, pieces):
+            wb = bytes_pool.tile([P, 4, K], U8, name="w_bytes")
+            w_bytes[j] = wb
+            rows = w_qk_bytes[N_TILE * j : N_TILE * (j + 1), :].rearrange("(a p) k -> p a k", p=P)
+            step = 4 // pieces
+            return [
+                (wb[:, step * i : step * (i + 1), :], rows[:, step * i : step * (i + 1), :]) for i in range(pieces)
+            ]
+
+        def start(moves):
+            for dst, src in moves:
+                nc.sync.dma_start(out=dst, in_=src)
+
+        def widen(j, a, pieces):
+            wf = wide_pool.tile([P, K], BF16, name="w_wide")
+            w_wide[(j, a)] = wf
+            kv = 512 * NVB[j][a // 2]
+            wb = w_bytes[j]
+            step = kv // pieces
+            for i in range(pieces):
+                cols = slice(step * i, step * (i + 1))
+                nc.vector.tensor_tensor(
+                    out=wf[:, cols], in0=wb[:, a, cols].bitcast(FP8), in1=scale_b[:, cols], op=ALU.mult
+                )
+            if kv < K:
+                nc.scalar.copy(out=wf[:, kv:K], in_=wb[:, a, kv:K].bitcast(FP8))
+
+        def turn_one(dst, words, g, u):
+            nc.tensor.transpose(dst, words[:, 256 * g + u : 256 * (g + 1) : 2], ident[:])
+
+        def turn_bank(xt, sources, g):
+            for i in range(2):
+                for u in range(2):
+                    turn_one(xt[:, u, P * i : P * (i + 1)], sources[i], g, u)
+
+        def empty_bank(xt, dst):
+            nc.scalar.copy(
+                out=dst.bitcast(F32).rearrange("p (c u) -> p c u", u=2),
+                in_=xt[:].rearrange("p u c -> p c u"),
+            )
+
+        def scaled_planes(pl, c0, bank, u, g):
+            n = bank.shape[1]
+            halves = bank.bitcast(BF16).rearrange("p (c e) -> p c e", e=2)
+            for e in range(2):
+                t = 2 * u + e
+                nc.scalar.activation(
+                    out=pl[:, t, c0 : c0 + n], in_=halves[:, :, e], func=ACT.Copy, scale=sc4[:, g, t : t + 1]
+                )
+
+        def interleave(dst, pl, c0, n):
+            nc.scalar.copy(
+                out=dst.rearrange("p (c i t) -> p c t i", i=4, t=4),
+                in_=pl[:, :, c0 : c0 + n].rearrange("p t (c i) -> p c t i", i=4),
+            )
+
+        def turn(j, g):
+            if g in (0, 2):
+                grp = grouped_pool.tile([P, 8 * N_TILE], BF16, name="grouped", align_bytes=64)
+                grouped[(j, g // 2)] = grp
+            if g == 4:
+                grp = grouped_pool.tile([P, 4 * N_TILE], BF16, name="grouped_last", bufs=2, align_bytes=64)
+                grouped[(j, 2)] = grp
+            grp = grouped[(j, g // 2)]
+            base = 2048 * (g % 2)
+            words = [w_wide[(j, a)][:].bitcast(F32) for a in range(4)]
+            if g >= max(NVB[j]):
+                pl = tmp_pool.tile([P, 4, N_TILE], BF16, name="planes")
+                for u in range(2):
+                    xt = psum_t.tile([P, 2, 256], F32, name="xt")
+                    flat = xt[:].rearrange("p u c -> p (u c)")
+                    for a in range(4):
+                        turn_one(flat[:, P * a : P * (a + 1)], words[a], g, u)
+                    scaled_planes(pl, 0, flat, u, g)
+                interleave(grp[:, base : base + 2048], pl, 0, N_TILE)
+                return
+            for b in range(2):
+                xt = psum_t.tile([P, 2, 256], F32, name="xt")
+                turn_bank(xt, words[2 * b : 2 * b + 2], g)
+                dst = grp[:, base + 1024 * b : base + 1024 * (b + 1)]
+                if g < NVB[j][b]:
+                    empty_bank(xt, dst)
+                else:
+                    pl = tmp_pool.tile([P, 4, N_TILE], BF16, name="planes")
+                    for u in range(2):
+                        scaled_planes(pl, 0, xt[:, u, :], u, g)
+                    interleave(dst, pl, 0, 256)
+
+        def quant(j, q):
+            width = N_TILE if q == 2 else 2 * N_TILE
+            cd = code_pool.tile([P, 2 * N_TILE], U32, name="cd", align_bytes=64)
+            sl = code_pool.tile([P, 2 * N_TILE], U8, name="sl", align_bytes=64)
+            codes[(j, q)] = (cd, sl)
+            nc.vector.quantize_mx(
+                out=cd[:, 0:width].bitcast(FP8X4), scales=sl[:, 0:width], in_=grouped[(j, q)][:]
+            )
+
+        def mult(j, g):
+            if g == 0:
+                acc0 = psum_a.tile([P, N_TILE], F32, name="acc0")
+                acc1 = psum_a.tile([P, N_TILE], F32, name="acc1")
+                acc[j] = (acc0, acc1)
+            cd, sl = codes[(j, g // 2)]
+            cols = slice(N_TILE * (g % 2), N_TILE * (g % 2 + 1))
+            for m in range(2):
+                nc.tensor.matmul_mx(
+                    out=acc[j][m][:],
+                    lhsT=h_codes[:, g, P * m : P * (m + 1)].bitcast(FP8X4),
+                    lhsT_scale=h_scales[:, g, P * m : P * (m + 1)],
+                    rhs=cd[:, cols].bitcast(FP8X4),
+                    rhs_scale=sl[:, cols],
+                    start=(g == 0),
+                    stop=(g == PASSES - 1),
+                )
+
+        def add_bias(j, m):
+            cols = slice(N_TILE * j, N_TILE * (j + 1))
+            nc.vector.tensor_tensor(out=x_out[:, m, cols], in0=acc[j][m][:], in1=bias_b[:, cols], op=ALU.add)
+
+        pending = {}
+
+        def rope_mul(j):
+            half, i = divmod(j, 5)
+            if i not in ROPE_AFTER:
+                return
+            at = ROPE_AFTER.index(i)
+            prev = ROPE_AFTER[at - 1] if at else -1
+            h0 = head_end(prev) if at else 0
+            h1 = head_end(i)
+            n = h1 - h0
+            xv = x_out[:, :, HALF * half + HEAD * h0 : HALF * half + HEAD * h1].rearrange(
+                "p m (h d) -> p m h d", d=HEAD
+            )
+            ta = tmp_pool.tile([P, 2, 13, ROT], F32, name="ta")
+            tb = tmp_pool.tile([P, 2, 13, ROT], F32, name="tb")
+            nc.vector.tensor_tensor(
+                out=ta[:, :, 0:n, :],
+                in0=xv[:, :, :, 0:ROT],
+                in1=cc[:].unsqueeze(2).to_broadcast([P, 2, n, ROT]),
+                op=ALU.mult,
+            )
+            nc.vector.tensor_tensor(
+                out=tb[:, :, 0:n, 0:16],
+                in0=xv[:, :, :, 16:32],
+                in1=ss[:, :, 0:16].unsqueeze(2).to_broadcast([P, 2, n, 16]),
+                op=ALU.mult,
+            )
+            nc.vector.tensor_tensor(
+                out=tb[:, :, 0:n, 16:32],
+                in0=xv[:, :, :, 0:16],
+                in1=ss[:, :, 16:32].unsqueeze(2).to_broadcast([P, 2, n, 16]),
+                op=ALU.mult,
+            )
+            pending[j] = (xv, ta, tb, n, prev, i, h0, h1, half)
+
+        def rope_add_and_store(j):
+            if j not in pending:
+                return
+            xv, ta, tb, n, prev, i, h0, h1, half = pending[j]
+            nc.vector.tensor_tensor(
+                out=xv[:, :, :, 0:ROT], in0=ta[:, :, 0:n, :], in1=tb[:, :, 0:n, :], op=ALU.add
+            )
+            c0 = min(N_TILE * (prev + 1), HEAD * h0)
+            c1 = min(N_TILE * (i + 1), HEAD * h1)
+            dram = (out_0, out_1)[half].rearrange("(m p) h d -> p m (h d)", p=P)
+            nc.sync.dma_start(out=dram[:, :, c0:c1], in_=x_out[:, :, HALF * half + c0 : HALF * half + c1])
+
+        flat_scale = w_qk_scale.rearrange("o k -> (o k)")
+        first = load(0, 4)
+
+        def scale_chunk(c):
+            nc.sync.dma_start(
+                out=scale_b[:, 512 * c : 512 * (c + 1)],
+                in_=flat_scale[512 * c : 512 * (c + 1)].partition_broadcast(P),
+            )
+
+        scale_chunk(0)
+        start(first[0:1])
+        for c in range(1, max(max(nv) for nv in NVB)):
+            scale_chunk(c)
+        start(first[1:4])
+        nc.sync.dma_start(out=h_sb[:], in_=hidden_states.rearrange("(m p) k -> p m k", p=P))
+        nc.sync.dma_start(out=sc4[:], in_=w_qk_scale.rearrange("o (g p t) -> p (o g) t", p=P, t=4))
+        start(load(1, 1))
+        start(load(2, 1))
+        nc.sync.dma_start(out=bias_b[:], in_=b_qk.partition_broadcast(P))
+        nc.sync.dma_start(out=cs_raw[:, :, 0, :], in_=cos.rearrange("(m p) j -> p m j", p=P))
+        nc.sync.dma_start(out=cs_raw[:, :, 1, :], in_=sin.rearrange("(m p) j -> p m j", p=P))
+
+        make_identity(nc, ident[:])
+        nc.vector.memset(junk[:, 0:1], 0.0)
+        nc.scalar.activation(out=junk[:, 1:2], in_=junk[:, 0:1], func=ACT.Copy)
+
+        h_words = [h_sb[:, m, :].bitcast(F32) for m in range(2)]
+        h_grouped = {}
+
+        def turn_hidden(g):
+            xt = psum_t.tile([P, 2, 256], F32, name="xt")
+            turn_bank(xt, h_words, g)
+            hg = grouped_pool.tile([P, 4 * TOKENS], BF16, name="h_grouped", bufs=5, align_bytes=64)
+            h_grouped[g] = hg
+            empty_bank(xt, hg[:])
+
+        def quant_hidden(g):
+            nc.vector.quantize_mx(
+                out=h_codes[:, g, :].bitcast(FP8X4), scales=h_scales[:, g, :], in_=h_grouped[g][:]
+            )
+
+        def tables():
+            nc.scalar.copy(out=cc[:, :, 0:16], in_=cs_raw[:, :, 0, :])
+            nc.scalar.copy(out=cc[:, :, 16:32], in_=cs_raw[:, :, 0, :])
+            nc.scalar.activation(out=ss[:, :, 0:16], in_=cs_raw[:, :, 1, :], func=ACT.Copy, scale=-1.0)
+            nc.scalar.copy(out=ss[:, :, 16:32], in_=cs_raw[:, :, 1, :])
+
+        for s in range(-2, TILES + 1):
+            for g in range(PASSES):
+                if s == -2:
+                    turn_hidden(g)
+                if 0 <= s + 1 < TILES:
+                    turn(s + 1, g)
+                if 0 <= s < TILES and g % 2 == 0:
+                    quant(s, g // 2)
+                if g == 0 and 0 <= s - 1 < TILES:
+                    mult(s - 1, PASSES - 1)
+                if g in (1, 3) and 0 <= s < TILES:
+                    mult(s, g - 1)
+                    mult(s, g)
+                if g < 4 and 0 <= s + 2 < TILES:
+                    widen(s + 2, g, NVB[0][0] if (s == -2 and g == 0) else 1)
+                if s == -1 and g == 4:
+                    for gg in range(PASSES):
+                        quant_hidden(gg)
+                    tables()
+                if 0 <= s - 1 < TILES:
+                    if g == 1:
+                        add_bias(s - 1, 0)
+                    if g == 2:
+                        add_bias(s - 1, 1)
+                    if g == 3:
+                        rope_mul(s - 1)
+                    if g == 4:
+                        rope_add_and_store(s - 1)
+                if g == 4 and 3 <= s + 2 + 3 < TILES:
+                    start(load(s + 2 + 3, 1))

@@ -18,6 +18,7 @@ K = 2560
 CHANNELS = 5120
 HALF = 2560
 HEAD = 80
+NH = 32
 ROT = 32
 PASSES = 5
 N_TILE = 512
@@ -123,12 +124,12 @@ def tile_flashphiattention_pa_kernel(
             )
 
         def turn(j, g):
-            if g in (0, 2):
-                grp = grouped_pool.tile([P, 8 * N_TILE], BF16, name="grouped", align_bytes=64)
+            if (j, g // 2) not in grouped:
+                if g < 4:
+                    grp = grouped_pool.tile([P, 8 * N_TILE], BF16, name="grouped", align_bytes=64)
+                else:
+                    grp = grouped_pool.tile([P, 4 * N_TILE], BF16, name="grouped_last", bufs=2, align_bytes=64)
                 grouped[(j, g // 2)] = grp
-            if g == 4:
-                grp = grouped_pool.tile([P, 4 * N_TILE], BF16, name="grouped_last", bufs=2, align_bytes=64)
-                grouped[(j, 2)] = grp
             grp = grouped[(j, g // 2)]
             base = 2048 * (g % 2)
             words = [w_wide[(j, a)][:].bitcast(F32) for a in range(4)]
@@ -233,8 +234,43 @@ def tile_flashphiattention_pa_kernel(
             dram = (out_0, out_1)[half].rearrange("(m p) h d -> p m (h d)", p=P)
             nc.sync.dma_start(out=dram[:, :, c0:c1], in_=x_out[:, :, HALF * half + c0 : HALF * half + c1])
 
+        def last_heads():
+            h0 = head_end(3)
+            n = NH - h0
+            c0 = HEAD * h0
+            ta = tmp_pool.tile([P, 2, 13, ROT], F32, name="ta")
+            tb = tmp_pool.tile([P, 2, 13, ROT], F32, name="tb")
+            for m in range(2):
+                xv = x_out[:, m, HALF + c0 : 2 * HALF].rearrange("p (h d) -> p h d", d=HEAD)
+                nc.vector.tensor_tensor(
+                    out=ta[:, m, 0:n, :],
+                    in0=xv[:, :, 0:ROT],
+                    in1=cc[:, m, :].unsqueeze(1).to_broadcast([P, n, ROT]),
+                    op=ALU.mult,
+                )
+                nc.vector.tensor_tensor(
+                    out=tb[:, m, 0:n, 0:16],
+                    in0=xv[:, :, 16:32],
+                    in1=ss[:, m, 0:16].unsqueeze(1).to_broadcast([P, n, 16]),
+                    op=ALU.mult,
+                )
+                nc.vector.tensor_tensor(
+                    out=tb[:, m, 0:n, 16:32],
+                    in0=xv[:, :, 0:16],
+                    in1=ss[:, m, 16:32].unsqueeze(1).to_broadcast([P, n, 16]),
+                    op=ALU.mult,
+                )
+                nc.vector.tensor_tensor(
+                    out=xv[:, :, 0:ROT], in0=ta[:, m, 0:n, :], in1=tb[:, m, 0:n, :], op=ALU.add
+                )
+                s0 = N_TILE * 4
+                dram = out_1.rearrange("(m p) h d -> p m (h d)", p=P)
+                nc.sync.dma_start(out=dram[:, m, s0:HALF], in_=x_out[:, m, HALF + s0 : 2 * HALF])
+
         flat_scale = w_qk_scale.rearrange("o k -> (o k)")
-        first = load(0, 4)
+        first = bytes_pool.tile([P, 4, K], U8, name="w_bytes")
+        w_bytes[0] = first
+        first_rows = w_qk_bytes[0:N_TILE, :].rearrange("(a p) k -> p a k", p=P)
 
         def scale_chunk(c):
             nc.sync.dma_start(
@@ -242,14 +278,25 @@ def tile_flashphiattention_pa_kernel(
                 in_=flat_scale[512 * c : 512 * (c + 1)].partition_broadcast(P),
             )
 
+        def first_chunk(c, a0, a1):
+            cols = slice(512 * c, 512 * (c + 1))
+            nc.sync.dma_start(out=first[:, a0:a1, cols], in_=first_rows[:, a0:a1, cols])
+
+        first_chunk(0, 0, 1)
         scale_chunk(0)
-        start(first[0:1])
-        for c in range(1, max(max(nv) for nv in NVB)):
-            scale_chunk(c)
-        start(first[1:4])
-        nc.sync.dma_start(out=h_sb[:], in_=hidden_states.rearrange("(m p) k -> p m k", p=P))
+        first_chunk(0, 1, 4)
+        scale_chunk(1)
+        first_chunk(1, 0, 4)
+        first_chunk(4, 0, 4)
+        scale_chunk(2)
+        first_chunk(2, 0, 4)
         nc.sync.dma_start(out=sc4[:], in_=w_qk_scale.rearrange("o (g p t) -> p (o g) t", p=P, t=4))
-        start(load(1, 1))
+        scale_chunk(3)
+        first_chunk(3, 0, 4)
+        second = load(1, 4)
+        start(second[0:1])
+        nc.sync.dma_start(out=h_sb[:], in_=hidden_states.rearrange("(m p) k -> p m k", p=P))
+        start(second[1:4])
         start(load(2, 1))
         nc.sync.dma_start(out=bias_b[:], in_=b_qk.partition_broadcast(P))
         nc.sync.dma_start(out=cs_raw[:, :, 0, :], in_=cos.rearrange("(m p) j -> p m j", p=P))
@@ -260,18 +307,18 @@ def tile_flashphiattention_pa_kernel(
         nc.scalar.activation(out=junk[:, 1:2], in_=junk[:, 0:1], func=ACT.Copy)
 
         h_words = [h_sb[:, m, :].bitcast(F32) for m in range(2)]
-        h_grouped = {}
+        h_grouped = const.tile([P, PASSES, 4 * TOKENS], BF16, name="h_grouped", align_bytes=64)
 
         def turn_hidden(g):
             xt = psum_t.tile([P, 2, 256], F32, name="xt")
             turn_bank(xt, h_words, g)
-            hg = grouped_pool.tile([P, 4 * TOKENS], BF16, name="h_grouped", bufs=5, align_bytes=64)
-            h_grouped[g] = hg
-            empty_bank(xt, hg[:])
+            empty_bank(xt, h_grouped[:, g, :])
 
-        def quant_hidden(g):
+        def quant_hidden(g0, g1):
             nc.vector.quantize_mx(
-                out=h_codes[:, g, :].bitcast(FP8X4), scales=h_scales[:, g, :], in_=h_grouped[g][:]
+                out=h_codes[:, g0:g1, :].rearrange("p g n -> p (g n)").bitcast(FP8X4),
+                scales=h_scales[:, g0:g1, :].rearrange("p g n -> p (g n)"),
+                in_=h_grouped[:, g0:g1, :].rearrange("p g n -> p (g n)"),
             )
 
         def tables():
@@ -280,11 +327,28 @@ def tile_flashphiattention_pa_kernel(
             nc.scalar.activation(out=ss[:, :, 0:16], in_=cs_raw[:, :, 1, :], func=ACT.Copy, scale=-1.0)
             nc.scalar.copy(out=ss[:, :, 16:32], in_=cs_raw[:, :, 1, :])
 
-        for s in range(-2, TILES + 1):
+        for a in range(4):
+            wf = wide_pool.tile([P, K], BF16, name="w_wide")
+            w_wide[(0, a)] = wf
+        for c in range(PASSES - 1):
+            cols = slice(512 * c, 512 * (c + 1))
+            for a in range(4):
+                nc.vector.tensor_tensor(
+                    out=w_wide[(0, a)][:, cols],
+                    in0=first[:, a, cols].bitcast(FP8),
+                    in1=scale_b[:, cols],
+                    op=ALU.mult,
+                )
+        for a in range(4):
+            nc.scalar.copy(out=w_wide[(0, a)][:, 2048:K], in_=first[:, a, 2048:K].bitcast(FP8))
+        turn(0, 4)
+        for g in range(PASSES):
+            turn_hidden(g)
+        start(load(3, 1))
+
+        for s in range(-1, TILES + 1):
             for g in range(PASSES):
-                if s == -2:
-                    turn_hidden(g)
-                if 0 <= s + 1 < TILES:
+                if 0 <= s + 1 < TILES and (s, g) != (-1, 4):
                     turn(s + 1, g)
                 if 0 <= s < TILES and g % 2 == 0:
                     quant(s, g // 2)
@@ -294,19 +358,21 @@ def tile_flashphiattention_pa_kernel(
                     mult(s, g - 1)
                     mult(s, g)
                 if g < 4 and 0 <= s + 2 < TILES:
-                    widen(s + 2, g, NVB[0][0] if (s == -2 and g == 0) else 1)
+                    widen(s + 2, g, 1)
                 if s == -1 and g == 4:
-                    for gg in range(PASSES):
-                        quant_hidden(gg)
+                    quant_hidden(0, 4)
+                    quant_hidden(4, 5)
                     tables()
                 if 0 <= s - 1 < TILES:
                     if g == 1:
                         add_bias(s - 1, 0)
                     if g == 2:
                         add_bias(s - 1, 1)
-                    if g == 3:
+                    if g == 3 and s < TILES:
                         rope_mul(s - 1)
-                    if g == 4:
+                    if g == 4 and s < TILES:
                         rope_add_and_store(s - 1)
-                if g == 4 and 3 <= s + 2 + 3 < TILES:
+                    if g == 4 and s == TILES:
+                        last_heads()
+                if g == 4 and 4 <= s + 2 + 3 < TILES:
                     start(load(s + 2 + 3, 1))

@@ -25,7 +25,7 @@ N_TILE = 512
 TILES = 10
 FLOPS = 2 * TOKENS * K * CHANNELS
 
-NVB = [(4, 4), (4, 3)] * 5
+NVB = [(4, 4), (4, 3), (4, 3), (4, 4), (4, 3), (4, 3), (4, 4), (4, 3), (4, 3), (4, 4)]
 ROPE_AFTER = [1, 3, 4]
 
 

from contextlib import ExitStack

import concourse.mybir as mybir
from concourse.masks import make_identity

F32 = mybir.dt.float32
BF16 = mybir.dt.bfloat16
U32 = mybir.dt.uint32
U8 = mybir.dt.uint8
FP8 = mybir.dt.float8_e4m3fn
FP8X4 = mybir.dt.float8_e4m3fn_x4
ALU = mybir.AluOpType
ACT = mybir.ActivationFunctionType

P = 128
TOKENS = 256
K = 2560
CHANNELS = 5120
HALF = 2560
HEAD = 80
NH = 32
ROT = 32
PASSES = 5
N_TILE = 512
TILES = 10
FLOPS = 2 * TOKENS * K * CHANNELS

NVB = [(4, 4), (4, 3), (4, 3), (4, 4), (4, 3), (4, 3), (4, 4), (4, 3), (4, 3), (4, 4)]
ROPE_AFTER = [1, 3, 4]


def head_end(i):
    return (N_TILE * (i + 1) - ROT) // HEAD + 1


def tile_flashphiattention_pa_kernel(
    tc, hidden_states, cos, sin, w_qk_bytes, w_qk_scale, b_qk, out_0, out_1
):
    nc = tc.nc
    with ExitStack() as ctx:
        const = ctx.enter_context(tc.tile_pool(name="const", bufs=1))
        bytes_pool = ctx.enter_context(tc.tile_pool(name="bytes", bufs=3))
        wide_pool = ctx.enter_context(tc.tile_pool(name="wide", bufs=8))
        grouped_pool = ctx.enter_context(tc.tile_pool(name="grouped", bufs=4))
        code_pool = ctx.enter_context(tc.tile_pool(name="codes", bufs=3))
        tmp_pool = ctx.enter_context(tc.tile_pool(name="tmp", bufs=2))
        psum_t = ctx.enter_context(tc.psum_pool(name="psum_t", bufs=4))
        psum_a = ctx.enter_context(tc.psum_pool(name="psum_a", bufs=2))
        ctx.enter_context(tc.manual_schedule(engines={mybir.EngineType.SP}))

        scale_b = const.tile([P, K], F32, name="scale_b")
        sc4 = const.tile([P, PASSES, 4], F32, name="sc4")
        bias_b = const.tile([P, CHANNELS], BF16, name="bias_b")
        cs_raw = const.tile([P, 2, 2, 16], BF16, name="cs_raw")
        cc = const.tile([P, 2, ROT], F32, name="cc")
        ss = const.tile([P, 2, ROT], F32, name="ss")
        ident = const.tile([P, P], F32, name="ident")
        junk = const.tile([P, 2], F32, name="junk")
        h_sb = const.tile([P, 2, K], BF16, name="h_sb")
        h_codes = const.tile([P, PASSES, TOKENS], U32, name="h_codes", align_bytes=64)
        h_scales = const.tile([P, PASSES, TOKENS], U8, name="h_scales", align_bytes=64)
        x_out = const.tile([P, 2, CHANNELS], F32, name="x_out")

        w_bytes = {}
        w_wide = {}
        grouped = {}
        codes = {}
        acc = {}

        def load(j, pieces):
            wb = bytes_pool.tile([P, 4, K], U8, name="w_bytes")
            w_bytes[j] = wb
            rows = w_qk_bytes[N_TILE * j : N_TILE * (j + 1), :].rearrange("(a p) k -> p a k", p=P)
            step = 4 // pieces
            return [
                (wb[:, step * i : step * (i + 1), :], rows[:, step * i : step * (i + 1), :]) for i in range(pieces)
            ]

        def start(moves):
            for dst, src in moves:
                nc.sync.dma_start(out=dst, in_=src)

        def widen(j, a, pieces):
            wf = wide_pool.tile([P, K], BF16, name="w_wide")
            w_wide[(j, a)] = wf
            kv = 512 * NVB[j][a // 2]
            wb = w_bytes[j]
            step = kv // pieces
            for i in range(pieces):
                cols = slice(step * i, step * (i + 1))
                nc.vector.tensor_tensor(
                    out=wf[:, cols], in0=wb[:, a, cols].bitcast(FP8), in1=scale_b[:, cols], op=ALU.mult
                )
            if kv < K:
                nc.scalar.copy(out=wf[:, kv:K], in_=wb[:, a, kv:K].bitcast(FP8))

        def turn_one(dst, words, g, u):
            nc.tensor.transpose(dst, words[:, 256 * g + u : 256 * (g + 1) : 2], ident[:])

        def turn_bank(xt, sources, g):
            for i in range(2):
                for u in range(2):
                    turn_one(xt[:, u, P * i : P * (i + 1)], sources[i], g, u)

        def empty_bank(xt, dst):
            nc.scalar.copy(
                out=dst.bitcast(F32).rearrange("p (c u) -> p c u", u=2),
                in_=xt[:].rearrange("p u c -> p c u"),
            )

        def scaled_planes(pl, c0, bank, u, g):
            n = bank.shape[1]
            halves = bank.bitcast(BF16).rearrange("p (c e) -> p c e", e=2)
            for e in range(2):
                t = 2 * u + e
                nc.scalar.activation(
                    out=pl[:, t, c0 : c0 + n], in_=halves[:, :, e], func=ACT.Copy, scale=sc4[:, g, t : t + 1]
                )

        def interleave(dst, pl, c0, n):
            nc.scalar.copy(
                out=dst.rearrange("p (c i t) -> p c t i", i=4, t=4),
                in_=pl[:, :, c0 : c0 + n].rearrange("p t (c i) -> p c t i", i=4),
            )

        def turn(j, g):
            if (j, g // 2) not in grouped:
                if g < 4:
                    grp = grouped_pool.tile([P, 8 * N_TILE], BF16, name="grouped", align_bytes=64)
                else:
                    grp = grouped_pool.tile([P, 4 * N_TILE], BF16, name="grouped_last", bufs=2, align_bytes=64)
                grouped[(j, g // 2)] = grp
            grp = grouped[(j, g // 2)]
            base = 2048 * (g % 2)
            words = [w_wide[(j, a)][:].bitcast(F32) for a in range(4)]
            if g >= max(NVB[j]):
                pl = tmp_pool.tile([P, 4, N_TILE], BF16, name="planes")
                for u in range(2):
                    xt = psum_t.tile([P, 2, 256], F32, name="xt")
                    flat = xt[:].rearrange("p u c -> p (u c)")
                    for a in range(4):
                        turn_one(flat[:, P * a : P * (a + 1)], words[a], g, u)
                    scaled_planes(pl, 0, flat, u, g)
                interleave(grp[:, base : base + 2048], pl, 0, N_TILE)
                return
            for b in range(2):
                xt = psum_t.tile([P, 2, 256], F32, name="xt")
                turn_bank(xt, words[2 * b : 2 * b + 2], g)
                dst = grp[:, base + 1024 * b : base + 1024 * (b + 1)]
                if g < NVB[j][b]:
                    empty_bank(xt, dst)
                else:
                    pl = tmp_pool.tile([P, 4, N_TILE], BF16, name="planes")
                    for u in range(2):
                        scaled_planes(pl, 0, xt[:, u, :], u, g)
                    interleave(dst, pl, 0, 256)

        def quant(j, q):
            width = N_TILE if q == 2 else 2 * N_TILE
            cd = code_pool.tile([P, 2 * N_TILE], U32, name="cd", align_bytes=64)
            sl = code_pool.tile([P, 2 * N_TILE], U8, name="sl", align_bytes=64)
            codes[(j, q)] = (cd, sl)
            nc.vector.quantize_mx(
                out=cd[:, 0:width].bitcast(FP8X4), scales=sl[:, 0:width], in_=grouped[(j, q)][:]
            )

        def mult(j, g):
            if g == 0:
                acc0 = psum_a.tile([P, N_TILE], F32, name="acc0")
                acc1 = psum_a.tile([P, N_TILE], F32, name="acc1")
                acc[j] = (acc0, acc1)
            cd, sl = codes[(j, g // 2)]
            cols = slice(N_TILE * (g % 2), N_TILE * (g % 2 + 1))
            for m in range(2):
                nc.tensor.matmul_mx(
                    out=acc[j][m][:],
                    lhsT=h_codes[:, g, P * m : P * (m + 1)].bitcast(FP8X4),
                    lhsT_scale=h_scales[:, g, P * m : P * (m + 1)],
                    rhs=cd[:, cols].bitcast(FP8X4),
                    rhs_scale=sl[:, cols],
                    start=(g == 0),
                    stop=(g == PASSES - 1),
                )

        def add_bias(j, m):
            cols = slice(N_TILE * j, N_TILE * (j + 1))
            nc.vector.tensor_tensor(out=x_out[:, m, cols], in0=acc[j][m][:], in1=bias_b[:, cols], op=ALU.add)

        pending = {}

        def rope_mul(j):
            half, i = divmod(j, 5)
            if i not in ROPE_AFTER:
                return
            at = ROPE_AFTER.index(i)
            prev = ROPE_AFTER[at - 1] if at else -1
            h0 = head_end(prev) if at else 0
            h1 = head_end(i)
            n = h1 - h0
            xv = x_out[:, :, HALF * half + HEAD * h0 : HALF * half + HEAD * h1].rearrange(
                "p m (h d) -> p m h d", d=HEAD
            )
            ta = tmp_pool.tile([P, 2, 13, ROT], F32, name="ta")
            tb = tmp_pool.tile([P, 2, 13, ROT], F32, name="tb")
            nc.vector.tensor_tensor(
                out=ta[:, :, 0:n, :],
                in0=xv[:, :, :, 0:ROT],
                in1=cc[:].unsqueeze(2).to_broadcast([P, 2, n, ROT]),
                op=ALU.mult,
            )
            nc.vector.tensor_tensor(
                out=tb[:, :, 0:n, 0:16],
                in0=xv[:, :, :, 16:32],
                in1=ss[:, :, 0:16].unsqueeze(2).to_broadcast([P, 2, n, 16]),
                op=ALU.mult,
            )
            nc.vector.tensor_tensor(
                out=tb[:, :, 0:n, 16:32],
                in0=xv[:, :, :, 0:16],
                in1=ss[:, :, 16:32].unsqueeze(2).to_broadcast([P, 2, n, 16]),
                op=ALU.mult,
            )
            pending[j] = (xv, ta, tb, n, prev, i, h0, h1, half)

        def rope_add_and_store(j):
            if j not in pending:
                return
            xv, ta, tb, n, prev, i, h0, h1, half = pending[j]
            nc.vector.tensor_tensor(
                out=xv[:, :, :, 0:ROT], in0=ta[:, :, 0:n, :], in1=tb[:, :, 0:n, :], op=ALU.add
            )
            c0 = min(N_TILE * (prev + 1), HEAD * h0)
            c1 = min(N_TILE * (i + 1), HEAD * h1)
            dram = (out_0, out_1)[half].rearrange("(m p) h d -> p m (h d)", p=P)
            nc.sync.dma_start(out=dram[:, :, c0:c1], in_=x_out[:, :, HALF * half + c0 : HALF * half + c1])

        def last_heads():
            h0 = head_end(3)
            n = NH - h0
            c0 = HEAD * h0
            ta = tmp_pool.tile([P, 2, 13, ROT], F32, name="ta")
            tb = tmp_pool.tile([P, 2, 13, ROT], F32, name="tb")
            for m in range(2):
                xv = x_out[:, m, HALF + c0 : 2 * HALF].rearrange("p (h d) -> p h d", d=HEAD)
                nc.vector.tensor_tensor(
                    out=ta[:, m, 0:n, :],
                    in0=xv[:, :, 0:ROT],
                    in1=cc[:, m, :].unsqueeze(1).to_broadcast([P, n, ROT]),
                    op=ALU.mult,
                )
                nc.vector.tensor_tensor(
                    out=tb[:, m, 0:n, 0:16],
                    in0=xv[:, :, 16:32],
                    in1=ss[:, m, 0:16].unsqueeze(1).to_broadcast([P, n, 16]),
                    op=ALU.mult,
                )
                nc.vector.tensor_tensor(
                    out=tb[:, m, 0:n, 16:32],
                    in0=xv[:, :, 0:16],
                    in1=ss[:, m, 16:32].unsqueeze(1).to_broadcast([P, n, 16]),
                    op=ALU.mult,
                )
                nc.vector.tensor_tensor(
                    out=xv[:, :, 0:ROT], in0=ta[:, m, 0:n, :], in1=tb[:, m, 0:n, :], op=ALU.add
                )
                s0 = N_TILE * 4
                dram = out_1.rearrange("(m p) h d -> p m (h d)", p=P)
                nc.sync.dma_start(out=dram[:, m, s0:HALF], in_=x_out[:, m, HALF + s0 : 2 * HALF])

        flat_scale = w_qk_scale.rearrange("o k -> (o k)")
        first = bytes_pool.tile([P, 4, K], U8, name="w_bytes")
        w_bytes[0] = first
        first_rows = w_qk_bytes[0:N_TILE, :].rearrange("(a p) k -> p a k", p=P)

        def scale_chunk(c):
            nc.sync.dma_start(
                out=scale_b[:, 512 * c : 512 * (c + 1)],
                in_=flat_scale[512 * c : 512 * (c + 1)].partition_broadcast(P),
            )

        def first_chunk(c, a0, a1):
            cols = slice(512 * c, 512 * (c + 1))
            nc.sync.dma_start(out=first[:, a0:a1, cols], in_=first_rows[:, a0:a1, cols])

        first_chunk(0, 0, 1)
        scale_chunk(0)
        first_chunk(0, 1, 4)
        scale_chunk(1)
        first_chunk(1, 0, 4)
        first_chunk(4, 0, 4)
        scale_chunk(2)
        first_chunk(2, 0, 4)
        nc.sync.dma_start(out=sc4[:], in_=w_qk_scale.rearrange("o (g p t) -> p (o g) t", p=P, t=4))
        scale_chunk(3)
        first_chunk(3, 0, 4)
        second = load(1, 4)
        start(second[0:1])
        nc.sync.dma_start(out=h_sb[:], in_=hidden_states.rearrange("(m p) k -> p m k", p=P))
        start(second[1:4])
        start(load(2, 1))
        nc.sync.dma_start(out=bias_b[:], in_=b_qk.partition_broadcast(P))
        nc.sync.dma_start(out=cs_raw[:, :, 0, :], in_=cos.rearrange("(m p) j -> p m j", p=P))
        nc.sync.dma_start(out=cs_raw[:, :, 1, :], in_=sin.rearrange("(m p) j -> p m j", p=P))

        make_identity(nc, ident[:])
        nc.vector.memset(junk[:, 0:1], 0.0)
        nc.scalar.activation(out=junk[:, 1:2], in_=junk[:, 0:1], func=ACT.Copy)

        h_words = [h_sb[:, m, :].bitcast(F32) for m in range(2)]
        h_grouped = const.tile([P, PASSES, 4 * TOKENS], BF16, name="h_grouped", align_bytes=64)

        def turn_hidden(g):
            xt = psum_t.tile([P, 2, 256], F32, name="xt")
            turn_bank(xt, h_words, g)
            empty_bank(xt, h_grouped[:, g, :])

        def quant_hidden(g0, g1):
            nc.vector.quantize_mx(
                out=h_codes[:, g0:g1, :].rearrange("p g n -> p (g n)").bitcast(FP8X4),
                scales=h_scales[:, g0:g1, :].rearrange("p g n -> p (g n)"),
                in_=h_grouped[:, g0:g1, :].rearrange("p g n -> p (g n)"),
            )

        def tables():
            nc.scalar.copy(out=cc[:, :, 0:16], in_=cs_raw[:, :, 0, :])
            nc.scalar.copy(out=cc[:, :, 16:32], in_=cs_raw[:, :, 0, :])
            nc.scalar.activation(out=ss[:, :, 0:16], in_=cs_raw[:, :, 1, :], func=ACT.Copy, scale=-1.0)
            nc.scalar.copy(out=ss[:, :, 16:32], in_=cs_raw[:, :, 1, :])

        for a in range(4):
            wf = wide_pool.tile([P, K], BF16, name="w_wide")
            w_wide[(0, a)] = wf
        for c in range(PASSES - 1):
            cols = slice(512 * c, 512 * (c + 1))
            for a in range(4):
                nc.vector.tensor_tensor(
                    out=w_wide[(0, a)][:, cols],
                    in0=first[:, a, cols].bitcast(FP8),
                    in1=scale_b[:, cols],
                    op=ALU.mult,
                )
        for a in range(4):
            nc.scalar.copy(out=w_wide[(0, a)][:, 2048:K], in_=first[:, a, 2048:K].bitcast(FP8))
        turn(0, 4)
        for g in range(PASSES):
            turn_hidden(g)
        start(load(3, 1))

        for s in range(-1, TILES + 1):
            for g in range(PASSES):
                if 0 <= s + 1 < TILES and (s, g) != (-1, 4):
                    turn(s + 1, g)
                if 0 <= s < TILES and g % 2 == 0:
                    quant(s, g // 2)
                if g == 0 and 0 <= s - 1 < TILES:
                    mult(s - 1, PASSES - 1)
                if g in (1, 3) and 0 <= s < TILES:
                    mult(s, g - 1)
                    mult(s, g)
                if g < 4 and 0 <= s + 2 < TILES:
                    widen(s + 2, g, 1)
                if s == -1 and g == 4:
                    quant_hidden(0, 4)
                    quant_hidden(4, 5)
                    tables()
                if 0 <= s - 1 < TILES:
                    if g == 1:
                        add_bias(s - 1, 0)
                    if g == 2:
                        add_bias(s - 1, 1)
                    if g == 3 and s < TILES:
                        rope_mul(s - 1)
                    if g == 4 and s < TILES:
                        rope_add_and_store(s - 1)
                    if g == 4 and s == TILES:
                        last_heads()
                if g == 4 and 4 <= s + 2 + 3 < TILES:
                    start(load(s + 2 + 3, 1))
